import numpy as np
import ml_dtypes


def mxq(x, axis, fmt="e4m3"):
    dtype, down = {"e4m3": (ml_dtypes.float8_e4m3fn, 7), "e5m2": (ml_dtypes.float8_e5m2, 14)}[fmt]
    v = np.moveaxis(np.asarray(x, np.float32).astype(ml_dtypes.bfloat16).astype(np.float64), axis, -1)
    blocks = v.reshape(v.shape[:-1] + (-1, 32))
    amax = np.abs(blocks).max(-1, keepdims=True)
    byte = np.maximum(np.where(amax > 0, np.frexp(amax)[1] - 1 + 127, 0) - down, 1)
    scale = np.exp2(byte - 127.0)
    codes = (blocks / scale).astype(np.float32).astype(dtype).astype(np.float64)
    return np.moveaxis((codes * scale).reshape(v.shape), -1, axis)


WIDE = False


def mx_kscale(k):
    if not WIDE:
        return np.ones(k)
    levels = np.array([10, -10, 5, -5, 0])
    a = np.random.permutation(np.resize(levels, k // 512 * 4)).reshape(k // 512, 4)
    idx = np.arange(k)
    return np.exp2(a[idx // 512, idx % 128 // 32])


BF16 = ml_dtypes.bfloat16


def bf(x):
    return np.asarray(x, np.float32).astype(BF16)


def f64(x):
    return np.asarray(x).astype(np.float64)


B, S, H, D, M = 2, 4096, 4, 128, 1024
E = H * D
R = B * S
EPS = 1e-6


def setup_inputs():
    s = mx_kscale(E)
    return {"query_input": bf(np.random.standard_normal((B, S, E))),
            "norm_query_w": bf((1.0 + 0.1 * np.random.standard_normal(E)) * s),
            "W_in": bf(np.random.standard_normal((E, E)) / np.sqrt(E) / s[None, :])}


def reference(query_input, norm_query_w, W_in):
    x = f64(query_input).reshape(R, E)
    normed = x * (1.0 / np.sqrt(np.mean(x * x, 1, keepdims=True) + EPS))
    h = normed * f64(norm_query_w)
    return (mxq(h, 1, "e4m3") @ mxq(f64(W_in), 1, "e4m3").T).reshape(B, S, E)

@@ -1,0 +1,238 @@
+from contextlib import ExitStack
+
+import concourse.mybir as mybir
+from concourse.masks import make_identity
+
+FLOPS = 2 * 8192 * 512 * 512
+
+F32 = mybir.dt.float32
+BF16 = mybir.dt.bfloat16
+U32 = mybir.dt.uint32
+U8 = mybir.dt.uint8
+FP8X4 = mybir.dt.float8_e4m3fn_x4
+ACT = mybir.ActivationFunctionType
+ALU = mybir.AluOpType
+
+P = 128
+E = 512
+NT = 64
+CH = 8
+EPS = 1e-6
+
+
+def plan():
+    loads = [(0, 2), (2, 4), (4, 8)] + [(8 * c, 8 * c + 8) for c in range(1, 8)]
+    batches = [(0, 2), (2, 4)] + [(4 * c, 4 * c + 4) for c in range(1, 15)] + [(60, 62), (62, 64)]
+    stores = [(4 * s, 4 * s + 4) for s in range(15)] + [(60, 62), (62, 64)]
+    return loads, batches, stores
+
+
+def pipeline_order(nt, batches, stores, ls=5, lz=3, vmod=16, vset=(1, 3, 5, 7, 9, 11, 13), tail_s=12, tail_v=2):
+    npair = nt // 2
+    batch_end = dict((e - 1, n) for n, (s, e) in enumerate(batches))
+    store_end = dict((e - 1, n) for n, (s, e) in enumerate(stores))
+    ops = []
+
+    def o_eng(i):
+        if i >= nt - tail_v:
+            return "V" if i % 2 == 0 else "S"
+        if i >= nt - tail_s:
+            return "S"
+        return "V" if (i % vmod) in vset else "S"
+
+    for tau in range(-ls, npair + 2):
+        qs, qz, qt, qe, qq, qo = tau + ls, tau + lz, tau + 1, tau, tau - 1, tau - 2
+        for h in range(2):
+            if 0 <= qs < npair:
+                i = 2 * qs + h
+                ops.append(("S1", i, "S"))
+                if i in batch_end:
+                    ops.append(("SQ", batch_end[i], "S"))
+            if 0 <= qo < npair and o_eng(2 * qo + h) == "S":
+                ops.append(("O", 2 * qo + h, "S"))
+        if 0 <= qz < npair:
+            for h in range(2):
+                ops.append(("Z", 2 * qz + h, "G"))
+        if 0 <= qt < npair:
+            for h in range(2):
+                ops.append(("T", 2 * qt + h, "P"))
+        if 0 <= qe < npair:
+            ops.append(("E", 2 * qe, "V"))
+        if 0 <= qq < npair:
+            ops.append(("Q", qq, "V"))
+        if 0 <= qe < npair:
+            ops.append(("E", 2 * qe + 1, "V"))
+        if 0 <= qq < npair:
+            for h in range(2):
+                ops.append(("M", 2 * qq + h, "P"))
+        if 0 <= qo < npair:
+            for h in range(2):
+                if o_eng(2 * qo + h) == "V":
+                    ops.append(("O", 2 * qo + h, "V"))
+            for h in range(2):
+                if 2 * qo + h in store_end:
+                    ops.append(("ST", store_end[2 * qo + h], "D"))
+    return ops
+
+
+def group_of(groups):
+    where = {}
+    for n, (s, e) in enumerate(groups):
+        for i in range(s, e):
+            where[i] = (n, i - s)
+    return where
+
+
+def tile_hopfieldmemorylayer_pa_t_kernel(tc, query_input, norm_query_w, W_in, out):
+    nc = tc.nc
+    x_view = query_input.flatten_outer_dims().rearrange("(c p j) k -> c p j k", p=P, j=CH)
+    out_view = out.flatten_outer_dims().rearrange("(c p j) n -> c p j n", p=P, j=CH)
+    g_view = norm_query_w.rearrange("(t p) -> t p", p=P)
+    w_view = W_in.rearrange("(a p) k -> a p k", p=P)
+
+    LOADS, BATCHES, STORES = plan()
+    load_of = group_of(LOADS)
+    batch_of = group_of(BATCHES)
+    store_of = group_of(STORES)
+
+    with ExitStack() as ctx:
+        const = ctx.enter_context(tc.tile_pool(name="const", bufs=1))
+        zpool = ctx.enter_context(tc.tile_pool(name="zpool", bufs=8))
+        gpool = ctx.enter_context(tc.tile_pool(name="gpool", bufs=3))
+        opool = ctx.enter_context(tc.tile_pool(name="opool", bufs=6))
+        psum = ctx.enter_context(tc.psum_pool(name="psum", bufs=4))
+        ctx.enter_context(tc.manual_schedule())
+
+        x_sb = []
+        w_sb = []
+        for n, (s, e) in enumerate(LOADS):
+            x_sb.append(const.tile([P, e - s, E], BF16, name="x%d" % n))
+        for a in range(4):
+            w_sb.append(const.tile([P, E], BF16, name="w%d" % a))
+
+        def load_x(n):
+            s, e = LOADS[n]
+            c, j0 = divmod(s, CH)
+            nc.sync.dma_start(out=x_sb[n][:], in_=x_view[c][:, j0 : j0 + e - s, :])
+
+        load_x(0)
+        for a in range(4):
+            nc.sync.dma_start(out=w_sb[a][:], in_=w_view[a])
+        for n in range(1, len(LOADS)):
+            load_x(n)
+
+        eps = const.tile([P, 1], F32, name="eps")
+        warm = const.tile([P, 1], F32, name="warm")
+        gz = const.tile([P, P], BF16, name="gz")
+        g4 = const.tile([P, 4], F32, name="g4")
+        ident_b = const.tile([P, P], BF16, name="ident_b")
+        ident_f = const.tile([P, P], F32, name="ident_f")
+        junk = const.tile([P, E], BF16, name="junk")
+        nc.vector.memset(eps[:], EPS)
+        nc.vector.memset(gz[:], 0.0)
+        nc.scalar.dma_start(out=gz[0:4, :], in_=g_view)
+        nc.scalar.activation(out=warm[:], in_=eps[:], func=ACT.Abs_reciprocal_sqrt)
+        make_identity(nc, ident_b[:])
+        make_identity(nc, ident_f[:])
+
+        g_ps = psum.tile([P, P], BF16, name="g_ps", tag="zt")
+        nc.tensor.transpose(g_ps[:], gz[:], ident_b[:])
+        nc.vector.tensor_copy(out=g4[:], in_=g_ps[:, 0:4])
+
+        w_grp = const.tile([P, E, 4], BF16, name="w_grp", align_bytes=64)
+        w_codes = const.tile([P, E], U32, name="w_codes", align_bytes=64)
+        w_scales = const.tile([P, E], U8, name="w_scales", align_bytes=64)
+        for a in range(4):
+            w_ps = psum.tile([P, 4, P], BF16, name="w_ps", tag="ob")
+            for t in range(4):
+                nc.tensor.transpose(w_ps[:, t, :], w_sb[a][:, P * t : P * t + P], ident_b[:])
+            nc.vector.tensor_copy(
+                out=w_grp[:, P * a : P * a + P, :], in_=w_ps[:].rearrange("p t n -> p n t")
+            )
+        nc.vector.quantize_mx(
+            out=w_codes[:].bitcast(FP8X4),
+            scales=w_scales[:],
+            in_=w_grp[:].rearrange("p n t -> p (n t)"),
+        )
+
+        ss = []
+        rstd = []
+        for n, (s, e) in enumerate(BATCHES):
+            ss.append(const.tile([P, e - s], F32, name="ss%d" % n))
+            rstd.append(const.tile([P, e - s], F32, name="rstd%d" % n))
+        z_t = {}
+        zt_t = {}
+        grp_t = {}
+        code_t = {}
+        scale_t = {}
+        ob_t = {}
+        osb_t = {}
+        g_bc = g4[:].unsqueeze(1).to_broadcast([P, P, 4])
+
+        for kind, i, eng in pipeline_order(NT, BATCHES, STORES):
+            if kind == "S1":
+                n, j = load_of[i]
+                b, col = batch_of[i]
+                nc.scalar.activation(
+                    out=junk[:], in_=x_sb[n][:, j, :], func=ACT.Square,
+                    accum_out=ss[b][:, col : col + 1],
+                )
+            elif kind == "SQ":
+                nc.scalar.activation(
+                    out=rstd[i][:], in_=ss[i][:], func=ACT.Abs_reciprocal_sqrt,
+                    scale=1.0 / E, bias=eps[:],
+                )
+            elif kind == "Z":
+                n, j = load_of[i]
+                b, col = batch_of[i]
+                z_t[i] = zpool.tile([P, E], F32, name="z", tag="z")
+                nc.gpsimd.tensor_scalar(
+                    out=z_t[i][:], in0=x_sb[n][:, j, :],
+                    scalar1=rstd[b][:, col : col + 1], scalar2=1.0,
+                    op0=ALU.mult, op1=ALU.mult,
+                )
+            elif kind == "T":
+                zt_t[i] = psum.tile([P, 4, P], F32, name="zt", tag="zt")
+                for t in range(4):
+                    nc.tensor.transpose(zt_t[i][:, t, :], z_t[i][:, P * t : P * t + P], ident_f[:])
+            elif kind == "E":
+                q, h = divmod(i, 2)
+                if h == 0:
+                    grp_t[q] = gpool.tile([P, 2, P, 4], BF16, name="grp", tag="grp", align_bytes=64)
+                nc.vector.tensor_tensor(
+                    out=grp_t[q][:, h, :, :], in0=zt_t[i][:].rearrange("p t r -> p r t"),
+                    in1=g_bc, op=ALU.mult,
+                )
+            elif kind == "Q":
+                code_t[i] = gpool.tile([P, 2 * P], U32, name="codes", tag="codes", align_bytes=64)
+                scale_t[i] = gpool.tile([P, 2 * P], U8, name="scales", tag="scales", align_bytes=64)
+                nc.vector.quantize_mx(
+                    out=code_t[i][:].bitcast(FP8X4),
+                    scales=scale_t[i][:],
+                    in_=grp_t[i][:].rearrange("p a r t -> p (a r t)"),
+                )
+            elif kind == "M":
+                q, h = divmod(i, 2)
+                ob_t[i] = psum.tile([P, E], F32, name="ob", tag="ob")
+                nc.tensor.matmul_mx(
+                    out=ob_t[i][:],
+                    lhsT=code_t[q][:, P * h : P * h + P].bitcast(FP8X4),
+                    lhsT_scale=scale_t[q][:, P * h : P * h + P],
+                    rhs=w_codes[:].bitcast(FP8X4),
+                    rhs_scale=w_scales[:],
+                    start=True,
+                    stop=True,
+                )
+            elif kind == "O":
+                n, j = store_of[i]
+                if n not in osb_t:
+                    s, e = STORES[n]
+                    osb_t[n] = opool.tile([P, e - s, E], F32, name="osb", tag="osb")
+                if eng == "S":
+                    nc.scalar.copy(out=osb_t[n][:, j, :], in_=ob_t[i][:])
+                else:
+                    nc.vector.tensor_copy(out=osb_t[n][:, j, :], in_=ob_t[i][:])
+            elif kind == "ST":
+                s, e = STORES[i]
+                c, j0 = divmod(s, CH)
+                nc.sync.dma_start(out=out_view[c][:, j0 : j0 + e - s, :], in_=osb_t[i][:])

@@ -20,58 +20,81 @@ CH = 8
 EPS = 1e-6
 
 
-def plan():
-    loads = [(0, 2), (2, 4), (4, 8)] + [(8 * c, 8 * c + 8) for c in range(1, 8)]
-    batches = [(0, 2), (2, 4)] + [(4 * c, 4 * c + 4) for c in range(1, 15)] + [(60, 62), (62, 64)]
-    stores = [(4 * s, 4 * s + 4) for s in range(15)] + [(60, 62), (62, 64)]
-    return loads, batches, stores
+def ranges(sizes):
+    out = []
+    s = 0
+    for n in sizes:
+        out.append((s, s + n))
+        s += n
+    assert s == NT
+    return out
 
 
-def pipeline_order(nt, batches, stores, ls=5, lz=3, vmod=16, vset=(1, 3, 5, 7, 9, 11, 13), tail_s=12, tail_v=2):
+def share(phases):
+    picked = set()
+    acc = 0.0
+    start = 0
+    for end, fraction in phases:
+        for i in range(start, end):
+            acc += fraction
+            if acc >= 1.0:
+                acc -= 1.0
+                picked.add(i)
+        start = end
+    return picked
+
+
+def pipeline_order(nt, batches, stores, quants, o_on_v, z_on_v, ls=5, lz=3):
     npair = nt // 2
     batch_end = dict((e - 1, n) for n, (s, e) in enumerate(batches))
     store_end = dict((e - 1, n) for n, (s, e) in enumerate(stores))
+    quant_end = dict((e - 1, n) for n, (s, e) in enumerate(quants))
     ops = []
+    q_wait = []
+    m_wait = []
+    o_wait = []
 
-    def o_eng(i):
-        if i >= nt - tail_v:
-            return "V" if i % 2 == 0 else "S"
-        if i >= nt - tail_s:
-            return "S"
-        return "V" if (i % vmod) in vset else "S"
-
-    for tau in range(-ls, npair + 2):
-        qs, qz, qt, qe, qq, qo = tau + ls, tau + lz, tau + 1, tau, tau - 1, tau - 2
+    tau = -ls
+    while tau < npair or q_wait or m_wait or o_wait:
+        qs, qz, qt, qe = tau + ls, tau + lz, tau + 1, tau
+        o_now = o_wait.pop(0) if o_wait else None
         for h in range(2):
             if 0 <= qs < npair:
                 i = 2 * qs + h
                 ops.append(("S1", i, "S"))
                 if i in batch_end:
                     ops.append(("SQ", batch_end[i], "S"))
-            if 0 <= qo < npair and o_eng(2 * qo + h) == "S":
-                ops.append(("O", 2 * qo + h, "S"))
+            if o_now is not None and 2 * o_now + h not in o_on_v:
+                ops.append(("O", 2 * o_now + h, "S"))
         if 0 <= qz < npair:
             for h in range(2):
-                ops.append(("Z", 2 * qz + h, "G"))
+                ops.append(("Z", 2 * qz + h, "V" if 2 * qz + h in z_on_v else "G"))
         if 0 <= qt < npair:
             for h in range(2):
                 ops.append(("T", 2 * qt + h, "P"))
         if 0 <= qe < npair:
             ops.append(("E", 2 * qe, "V"))
-        if 0 <= qq < npair:
-            ops.append(("Q", qq, "V"))
+        if q_wait:
+            n = q_wait.pop(0)
+            ops.append(("Q", n, "V"))
+            m_wait.extend(range(quants[n][0] // 2, quants[n][1] // 2))
         if 0 <= qe < npair:
             ops.append(("E", 2 * qe + 1, "V"))
-        if 0 <= qq < npair:
+            if 2 * qe + 1 in quant_end:
+                q_wait.append(quant_end[2 * qe + 1])
+        if m_wait:
+            m = m_wait.pop(0)
             for h in range(2):
-                ops.append(("M", 2 * qq + h, "P"))
-        if 0 <= qo < npair:
+                ops.append(("M", 2 * m + h, "P"))
+            o_wait.append(m)
+        if o_now is not None:
             for h in range(2):
-                if o_eng(2 * qo + h) == "V":
-                    ops.append(("O", 2 * qo + h, "V"))
+                if 2 * o_now + h in o_on_v:
+                    ops.append(("O", 2 * o_now + h, "V"))
             for h in range(2):
-                if 2 * qo + h in store_end:
-                    ops.append(("ST", store_end[2 * qo + h], "D"))
+                if 2 * o_now + h in store_end:
+                    ops.append(("ST", store_end[2 * o_now + h], "D"))
+        tau += 1
     return ops
 
 
@@ -90,16 +113,22 @@ def tile_hopfieldmemorylayer_pa_t_kernel(tc, query_input, norm_query_w, W_in, ou
     g_view = norm_query_w.rearrange("(t p) -> t p", p=P)
     w_view = W_in.rearrange("(a p) k -> a p k", p=P)
 
-    LOADS, BATCHES, STORES = plan()
+    LOADS = ranges([2, 2, 4] + [8] * 7)
+    BATCHES = ranges([2, 2] + [4] * 14 + [2, 2])
+    QUANTS = ranges([4] * 15 + [2, 2])
+    STORES = ranges([4] * 12 + [2] * 8)
+    O_ON_V = share([(24, 0.3), (56, 0.4), (62, 0.3), (64, 0.5)])
+    Z_ON_V = set()
     load_of = group_of(LOADS)
     batch_of = group_of(BATCHES)
+    quant_of = group_of(QUANTS)
     store_of = group_of(STORES)
 
     with ExitStack() as ctx:
         const = ctx.enter_context(tc.tile_pool(name="const", bufs=1))
         zpool = ctx.enter_context(tc.tile_pool(name="zpool", bufs=8))
         gpool = ctx.enter_context(tc.tile_pool(name="gpool", bufs=3))
-        opool = ctx.enter_context(tc.tile_pool(name="opool", bufs=6))
+        opool = ctx.enter_context(tc.tile_pool(name="opool", bufs=8))
         psum = ctx.enter_context(tc.psum_pool(name="psum", bufs=4))
         ctx.enter_context(tc.manual_schedule())
 
@@ -169,7 +198,7 @@ def tile_hopfieldmemorylayer_pa_t_kernel(tc, query_input, norm_query_w, W_in, ou
         osb_t = {}
         g_bc = g4[:].unsqueeze(1).to_broadcast([P, P, 4])
 
-        for kind, i, eng in pipeline_order(NT, BATCHES, STORES):
+        for kind, i, eng in pipeline_order(NT, BATCHES, STORES, QUANTS, O_ON_V, Z_ON_V, ls=4, lz=2):
             if kind == "S1":
                 n, j = load_of[i]
                 b, col = batch_of[i]
@@ -186,38 +215,47 @@ def tile_hopfieldmemorylayer_pa_t_kernel(tc, query_input, norm_query_w, W_in, ou
                 n, j = load_of[i]
                 b, col = batch_of[i]
                 z_t[i] = zpool.tile([P, E], F32, name="z", tag="z")
-                nc.gpsimd.tensor_scalar(
-                    out=z_t[i][:], in0=x_sb[n][:, j, :],
-                    scalar1=rstd[b][:, col : col + 1], scalar2=1.0,
-                    op0=ALU.mult, op1=ALU.mult,
-                )
+                if eng == "G":
+                    nc.gpsimd.tensor_scalar(
+                        out=z_t[i][:], in0=x_sb[n][:, j, :],
+                        scalar1=rstd[b][:, col : col + 1], scalar2=1.0,
+                        op0=ALU.mult, op1=ALU.mult,
+                    )
+                else:
+                    nc.vector.tensor_scalar(
+                        out=z_t[i][:], in0=x_sb[n][:, j, :],
+                        scalar1=rstd[b][:, col : col + 1], scalar2=None,
+                        op0=ALU.mult,
+                    )
             elif kind == "T":
                 zt_t[i] = psum.tile([P, 4, P], F32, name="zt", tag="zt")
                 for t in range(4):
                     nc.tensor.transpose(zt_t[i][:, t, :], z_t[i][:, P * t : P * t + P], ident_f[:])
             elif kind == "E":
-                q, h = divmod(i, 2)
-                if h == 0:
-                    grp_t[q] = gpool.tile([P, 2, P, 4], BF16, name="grp", tag="grp", align_bytes=64)
+                n, j = quant_of[i]
+                if j == 0:
+                    s, e = QUANTS[n]
+                    grp_t[n] = gpool.tile([P, e - s, P, 4], BF16, name="grp", tag="grp", align_bytes=64)
                 nc.vector.tensor_tensor(
-                    out=grp_t[q][:, h, :, :], in0=zt_t[i][:].rearrange("p t r -> p r t"),
+                    out=grp_t[n][:, j, :, :], in0=zt_t[i][:].rearrange("p t r -> p r t"),
                     in1=g_bc, op=ALU.mult,
                 )
             elif kind == "Q":
-                code_t[i] = gpool.tile([P, 2 * P], U32, name="codes", tag="codes", align_bytes=64)
-                scale_t[i] = gpool.tile([P, 2 * P], U8, name="scales", tag="scales", align_bytes=64)
+                s, e = QUANTS[i]
+                code_t[i] = gpool.tile([P, (e - s) * P], U32, name="codes", tag="codes", align_bytes=64)
+                scale_t[i] = gpool.tile([P, (e - s) * P], U8, name="scales", tag="scales", align_bytes=64)
                 nc.vector.quantize_mx(
                     out=code_t[i][:].bitcast(FP8X4),
                     scales=scale_t[i][:],
                     in_=grp_t[i][:].rearrange("p a r t -> p (a r t)"),
                 )
             elif kind == "M":
-                q, h = divmod(i, 2)
+                n, j = quant_of[i]
                 ob_t[i] = psum.tile([P, E], F32, name="ob", tag="ob")
                 nc.tensor.matmul_mx(
                     out=ob_t[i][:],
-                    lhsT=code_t[q][:, P * h : P * h + P].bitcast(FP8X4),
-                    lhsT_scale=scale_t[q][:, P * h : P * h + P],
+                    lhsT=code_t[n][:, P * j : P * j + P].bitcast(FP8X4),
+                    lhsT_scale=scale_t[n][:, P * j : P * j + P],
                     rhs=w_codes[:].bitcast(FP8X4),
                     rhs_scale=w_scales[:],
                     start=True,

@@ -117,7 +117,7 @@ def tile_hopfieldmemorylayer_pa_t_kernel(tc, query_input, norm_query_w, W_in, ou
     BATCHES = ranges([2, 2] + [4] * 14 + [2, 2])
     QUANTS = ranges([4] * 15 + [2, 2])
     STORES = ranges([4] * 12 + [2] * 8)
-    O_ON_V = share([(24, 0.3), (56, 0.4), (62, 0.3), (64, 0.5)])
+    O_ON_V = share([(24, 0.5), (56, 0.5), (62, 0.4), (64, 0.5)])
     Z_ON_V = set()
     load_of = group_of(LOADS)
     batch_of = group_of(BATCHES)

@@ -117,7 +117,7 @@ def tile_hopfieldmemorylayer_pa_t_kernel(tc, query_input, norm_query_w, W_in, ou
     BATCHES = ranges([2, 2] + [4] * 14 + [2, 2])
     QUANTS = ranges([4] * 15 + [2, 2])
     STORES = ranges([4] * 12 + [2] * 8)
-    O_ON_V = share([(24, 0.5), (56, 0.5), (62, 0.4), (64, 0.5)])
+    O_ON_V = share([(24, 0.4), (56, 0.4), (62, 0.3), (64, 0.5)])
     Z_ON_V = set()
     load_of = group_of(LOADS)
     batch_of = group_of(BATCHES)
@@ -156,7 +156,7 @@ def tile_hopfieldmemorylayer_pa_t_kernel(tc, query_input, norm_query_w, W_in, ou
         g4 = const.tile([P, 4], F32, name="g4")
         ident_b = const.tile([P, P], BF16, name="ident_b")
         ident_f = const.tile([P, P], F32, name="ident_f")
-        junk = const.tile([P, E], BF16, name="junk")
+        junk = const.tile([P, 8, E], BF16, name="junk")
         nc.vector.memset(eps[:], EPS)
         nc.vector.memset(gz[:], 0.0)
         nc.scalar.dma_start(out=gz[0:4, :], in_=g_view)
@@ -203,7 +203,7 @@ def tile_hopfieldmemorylayer_pa_t_kernel(tc, query_input, norm_query_w, W_in, ou
                 n, j = load_of[i]
                 b, col = batch_of[i]
                 nc.scalar.activation(
-                    out=junk[:], in_=x_sb[n][:, j, :], func=ACT.Square,
+                    out=junk[:, i % 8, :], in_=x_sb[n][:, j, :], func=ACT.Square,
                     accum_out=ss[b][:, col : col + 1],
                 )
             elif kind == "SQ":

@@ -50,6 +50,7 @@ def pipeline_order(nt, batches, stores, quants, o_on_v, z_on_v, ls=5, lz=3):
     store_end = dict((e - 1, n) for n, (s, e) in enumerate(stores))
     quant_end = dict((e - 1, n) for n, (s, e) in enumerate(quants))
     ops = []
+    sq_wait = []
     q_wait = []
     m_wait = []
     o_wait = []
@@ -62,10 +63,17 @@ def pipeline_order(nt, batches, stores, quants, o_on_v, z_on_v, ls=5, lz=3):
             if 0 <= qs < npair:
                 i = 2 * qs + h
                 ops.append(("S1", i, "S"))
+                if sq_wait:
+                    ops.append(("SQ", sq_wait.pop(0), "S"))
                 if i in batch_end:
-                    ops.append(("SQ", batch_end[i], "S"))
-            if o_now is not None and 2 * o_now + h not in o_on_v:
-                ops.append(("O", 2 * o_now + h, "S"))
+                    if i < 8 or qs == npair - 1:
+                        ops.append(("SQ", batch_end[i], "S"))
+                    else:
+                        sq_wait.append(batch_end[i])
+            if o_now is not None and 2 * o_now + 1 - h not in o_on_v:
+                ops.append(("O", 2 * o_now + 1 - h, "S"))
+                if sq_wait:
+                    ops.append(("SQ", sq_wait.pop(0), "S"))
         if 0 <= qz < npair:
             for h in range(2):
                 ops.append(("Z", 2 * qz + h, "V" if 2 * qz + h in z_on_v else "G"))
@@ -73,13 +81,13 @@ def pipeline_order(nt, batches, stores, quants, o_on_v, z_on_v, ls=5, lz=3):
             for h in range(2):
                 ops.append(("T", 2 * qt + h, "P"))
         if 0 <= qe < npair:
-            ops.append(("E", 2 * qe, "V"))
+            ops.append(("E", 2 * qe + 1, "V"))
         if q_wait:
             n = q_wait.pop(0)
             ops.append(("Q", n, "V"))
             m_wait.extend(range(quants[n][0] // 2, quants[n][1] // 2))
         if 0 <= qe < npair:
-            ops.append(("E", 2 * qe + 1, "V"))
+            ops.append(("E", 2 * qe, "V"))
             if 2 * qe + 1 in quant_end:
                 q_wait.append(quant_end[2 * qe + 1])
         if m_wait:
@@ -88,7 +96,7 @@ def pipeline_order(nt, batches, stores, quants, o_on_v, z_on_v, ls=5, lz=3):
                 ops.append(("M", 2 * m + h, "P"))
             o_wait.append(m)
         if o_now is not None:
-            for h in range(2):
+            for h in (1, 0):
                 if 2 * o_now + h in o_on_v:
                     ops.append(("O", 2 * o_now + h, "V"))
             for h in range(2):
@@ -117,7 +125,7 @@ def tile_hopfieldmemorylayer_pa_t_kernel(tc, query_input, norm_query_w, W_in, ou
     BATCHES = ranges([2, 2] + [4] * 14 + [2, 2])
     QUANTS = ranges([4] * 15 + [2, 2])
     STORES = ranges([4] * 12 + [2] * 8)
-    O_ON_V = share([(24, 0.4), (56, 0.4), (62, 0.3), (64, 0.5)])
+    O_ON_V = share([(24, 0.45), (56, 0.45), (62, 0.3), (64, 0.5)])
     Z_ON_V = set()
     load_of = group_of(LOADS)
     batch_of = group_of(BATCHES)
@@ -156,7 +164,7 @@ def tile_hopfieldmemorylayer_pa_t_kernel(tc, query_input, norm_query_w, W_in, ou
         g4 = const.tile([P, 4], F32, name="g4")
         ident_b = const.tile([P, P], BF16, name="ident_b")
         ident_f = const.tile([P, P], F32, name="ident_f")
-        junk = const.tile([P, 8, E], BF16, name="junk")
+        junk = const.tile([P, 24, E], BF16, name="junk")
         nc.vector.memset(eps[:], EPS)
         nc.vector.memset(gz[:], 0.0)
         nc.scalar.dma_start(out=gz[0:4, :], in_=g_view)
@@ -203,7 +211,7 @@ def tile_hopfieldmemorylayer_pa_t_kernel(tc, query_input, norm_query_w, W_in, ou
                 n, j = load_of[i]
                 b, col = batch_of[i]
                 nc.scalar.activation(
-                    out=junk[:, i % 8, :], in_=x_sb[n][:, j, :], func=ACT.Square,
+                    out=junk[:, i % 24, :], in_=x_sb[n][:, j, :], func=ACT.Square,
                     accum_out=ss[b][:, col : col + 1],
                 )
             elif kind == "SQ":
@@ -233,7 +241,7 @@ def tile_hopfieldmemorylayer_pa_t_kernel(tc, query_input, norm_query_w, W_in, ou
                     nc.tensor.transpose(zt_t[i][:, t, :], z_t[i][:, P * t : P * t + P], ident_f[:])
             elif kind == "E":
                 n, j = quant_of[i]
-                if j == 0:
+                if n not in grp_t:
                     s, e = QUANTS[n]
                     grp_t[n] = gpool.tile([P, e - s, P, 4], BF16, name="grp", tag="grp", align_bytes=64)
                 nc.vector.tensor_tensor(

@@ -125,7 +125,7 @@ def tile_hopfieldmemorylayer_pa_t_kernel(tc, query_input, norm_query_w, W_in, ou
     BATCHES = ranges([2, 2] + [4] * 14 + [2, 2])
     QUANTS = ranges([4] * 15 + [2, 2])
     STORES = ranges([4] * 12 + [2] * 8)
-    O_ON_V = share([(24, 0.45), (56, 0.45), (62, 0.3), (64, 0.5)])
+    O_ON_V = share([(16, 0.6), (48, 0.55), (62, 0.0), (64, 0.5)])
     Z_ON_V = set()
     load_of = group_of(LOADS)
     batch_of = group_of(BATCHES)

from contextlib import ExitStack

import concourse.mybir as mybir
from concourse.masks import make_identity

FLOPS = 2 * 8192 * 512 * 512

F32 = mybir.dt.float32
BF16 = mybir.dt.bfloat16
U32 = mybir.dt.uint32
U8 = mybir.dt.uint8
FP8X4 = mybir.dt.float8_e4m3fn_x4
ACT = mybir.ActivationFunctionType
ALU = mybir.AluOpType

P = 128
E = 512
NT = 64
CH = 8
EPS = 1e-6


def ranges(sizes):
    out = []
    s = 0
    for n in sizes:
        out.append((s, s + n))
        s += n
    assert s == NT
    return out


def share(phases):
    picked = set()
    acc = 0.0
    start = 0
    for end, fraction in phases:
        for i in range(start, end):
            acc += fraction
            if acc >= 1.0:
                acc -= 1.0
                picked.add(i)
        start = end
    return picked


def pipeline_order(nt, batches, stores, quants, o_on_v, z_on_v, ls=5, lz=3):
    npair = nt // 2
    batch_end = dict((e - 1, n) for n, (s, e) in enumerate(batches))
    store_end = dict((e - 1, n) for n, (s, e) in enumerate(stores))
    quant_end = dict((e - 1, n) for n, (s, e) in enumerate(quants))
    ops = []
    sq_wait = []
    q_wait = []
    m_wait = []
    o_wait = []

    tau = -ls
    while tau < npair or q_wait or m_wait or o_wait:
        qs, qz, qt, qe = tau + ls, tau + lz, tau + 1, tau
        o_now = o_wait.pop(0) if o_wait else None
        for h in range(2):
            if 0 <= qs < npair:
                i = 2 * qs + h
                ops.append(("S1", i, "S"))
                if sq_wait:
                    ops.append(("SQ", sq_wait.pop(0), "S"))
                if i in batch_end:
                    if i < 8 or qs == npair - 1:
                        ops.append(("SQ", batch_end[i], "S"))
                    else:
                        sq_wait.append(batch_end[i])
            if o_now is not None and 2 * o_now + 1 - h not in o_on_v:
                ops.append(("O", 2 * o_now + 1 - h, "S"))
                if sq_wait:
                    ops.append(("SQ", sq_wait.pop(0), "S"))
        if 0 <= qz < npair:
            for h in range(2):
                ops.append(("Z", 2 * qz + h, "V" if 2 * qz + h in z_on_v else "G"))
        if 0 <= qt < npair:
            for h in range(2):
                ops.append(("T", 2 * qt + h, "P"))
        if 0 <= qe < npair:
            ops.append(("E", 2 * qe + 1, "V"))
        if q_wait:
            n = q_wait.pop(0)
            ops.append(("Q", n, "V"))
            m_wait.extend(range(quants[n][0] // 2, quants[n][1] // 2))
        if 0 <= qe < npair:
            ops.append(("E", 2 * qe, "V"))
            if 2 * qe + 1 in quant_end:
                q_wait.append(quant_end[2 * qe + 1])
        if m_wait:
            m = m_wait.pop(0)
            for h in range(2):
                ops.append(("M", 2 * m + h, "P"))
            o_wait.append(m)
        if o_now is not None:
            for h in (1, 0):
                if 2 * o_now + h in o_on_v:
                    ops.append(("O", 2 * o_now + h, "V"))
            for h in range(2):
                if 2 * o_now + h in store_end:
                    ops.append(("ST", store_end[2 * o_now + h], "D"))
        tau += 1
    return ops


def group_of(groups):
    where = {}
    for n, (s, e) in enumerate(groups):
        for i in range(s, e):
            where[i] = (n, i - s)
    return where


def tile_hopfieldmemorylayer_pa_t_kernel(tc, query_input, norm_query_w, W_in, out):
    nc = tc.nc
    x_view = query_input.flatten_outer_dims().rearrange("(c p j) k -> c p j k", p=P, j=CH)
    out_view = out.flatten_outer_dims().rearrange("(c p j) n -> c p j n", p=P, j=CH)
    g_view = norm_query_w.rearrange("(t p) -> t p", p=P)
    w_view = W_in.rearrange("(a p) k -> a p k", p=P)

    LOADS = ranges([2, 2, 4] + [8] * 7)
    BATCHES = ranges([2, 2] + [4] * 14 + [2, 2])
    QUANTS = ranges([4] * 15 + [2, 2])
    STORES = ranges([4] * 12 + [2] * 8)
    O_ON_V = share([(16, 0.6), (48, 0.55), (62, 0.0), (64, 0.5)])
    Z_ON_V = set()
    load_of = group_of(LOADS)
    batch_of = group_of(BATCHES)
    quant_of = group_of(QUANTS)
    store_of = group_of(STORES)

    with ExitStack() as ctx:
        const = ctx.enter_context(tc.tile_pool(name="const", bufs=1))
        zpool = ctx.enter_context(tc.tile_pool(name="zpool", bufs=8))
        gpool = ctx.enter_context(tc.tile_pool(name="gpool", bufs=3))
        opool = ctx.enter_context(tc.tile_pool(name="opool", bufs=8))
        psum = ctx.enter_context(tc.psum_pool(name="psum", bufs=4))
        ctx.enter_context(tc.manual_schedule())

        x_sb = []
        w_sb = []
        for n, (s, e) in enumerate(LOADS):
            x_sb.append(const.tile([P, e - s, E], BF16, name="x%d" % n))
        for a in range(4):
            w_sb.append(const.tile([P, E], BF16, name="w%d" % a))

        def load_x(n):
            s, e = LOADS[n]
            c, j0 = divmod(s, CH)
            nc.sync.dma_start(out=x_sb[n][:], in_=x_view[c][:, j0 : j0 + e - s, :])

        load_x(0)
        for a in range(4):
            nc.sync.dma_start(out=w_sb[a][:], in_=w_view[a])
        for n in range(1, len(LOADS)):
            load_x(n)

        eps = const.tile([P, 1], F32, name="eps")
        warm = const.tile([P, 1], F32, name="warm")
        gz = const.tile([P, P], BF16, name="gz")
        g4 = const.tile([P, 4], F32, name="g4")
        ident_b = const.tile([P, P], BF16, name="ident_b")
        ident_f = const.tile([P, P], F32, name="ident_f")
        junk = const.tile([P, 24, E], BF16, name="junk")
        nc.vector.memset(eps[:], EPS)
        nc.vector.memset(gz[:], 0.0)
        nc.scalar.dma_start(out=gz[0:4, :], in_=g_view)
        nc.scalar.activation(out=warm[:], in_=eps[:], func=ACT.Abs_reciprocal_sqrt)
        make_identity(nc, ident_b[:])
        make_identity(nc, ident_f[:])

        g_ps = psum.tile([P, P], BF16, name="g_ps", tag="zt")
        nc.tensor.transpose(g_ps[:], gz[:], ident_b[:])
        nc.vector.tensor_copy(out=g4[:], in_=g_ps[:, 0:4])

        w_grp = const.tile([P, E, 4], BF16, name="w_grp", align_bytes=64)
        w_codes = const.tile([P, E], U32, name="w_codes", align_bytes=64)
        w_scales = const.tile([P, E], U8, name="w_scales", align_bytes=64)
        for a in range(4):
            w_ps = psum.tile([P, 4, P], BF16, name="w_ps", tag="ob")
            for t in range(4):
                nc.tensor.transpose(w_ps[:, t, :], w_sb[a][:, P * t : P * t + P], ident_b[:])
            nc.vector.tensor_copy(
                out=w_grp[:, P * a : P * a + P, :], in_=w_ps[:].rearrange("p t n -> p n t")
            )
        nc.vector.quantize_mx(
            out=w_codes[:].bitcast(FP8X4),
            scales=w_scales[:],
            in_=w_grp[:].rearrange("p n t -> p (n t)"),
        )

        ss = []
        rstd = []
        for n, (s, e) in enumerate(BATCHES):
            ss.append(const.tile([P, e - s], F32, name="ss%d" % n))
            rstd.append(const.tile([P, e - s], F32, name="rstd%d" % n))
        z_t = {}
        zt_t = {}
        grp_t = {}
        code_t = {}
        scale_t = {}
        ob_t = {}
        osb_t = {}
        g_bc = g4[:].unsqueeze(1).to_broadcast([P, P, 4])

        for kind, i, eng in pipeline_order(NT, BATCHES, STORES, QUANTS, O_ON_V, Z_ON_V, ls=4, lz=2):
            if kind == "S1":
                n, j = load_of[i]
                b, col = batch_of[i]
                nc.scalar.activation(
                    out=junk[:, i % 24, :], in_=x_sb[n][:, j, :], func=ACT.Square,
                    accum_out=ss[b][:, col : col + 1],
                )
            elif kind == "SQ":
                nc.scalar.activation(
                    out=rstd[i][:], in_=ss[i][:], func=ACT.Abs_reciprocal_sqrt,
                    scale=1.0 / E, bias=eps[:],
                )
            elif kind == "Z":
                n, j = load_of[i]
                b, col = batch_of[i]
                z_t[i] = zpool.tile([P, E], F32, name="z", tag="z")
                if eng == "G":
                    nc.gpsimd.tensor_scalar(
                        out=z_t[i][:], in0=x_sb[n][:, j, :],
                        scalar1=rstd[b][:, col : col + 1], scalar2=1.0,
                        op0=ALU.mult, op1=ALU.mult,
                    )
                else:
                    nc.vector.tensor_scalar(
                        out=z_t[i][:], in0=x_sb[n][:, j, :],
                        scalar1=rstd[b][:, col : col + 1], scalar2=None,
                        op0=ALU.mult,
                    )
            elif kind == "T":
                zt_t[i] = psum.tile([P, 4, P], F32, name="zt", tag="zt")
                for t in range(4):
                    nc.tensor.transpose(zt_t[i][:, t, :], z_t[i][:, P * t : P * t + P], ident_f[:])
            elif kind == "E":
                n, j = quant_of[i]
                if n not in grp_t:
                    s, e = QUANTS[n]
                    grp_t[n] = gpool.tile([P, e - s, P, 4], BF16, name="grp", tag="grp", align_bytes=64)
                nc.vector.tensor_tensor(
                    out=grp_t[n][:, j, :, :], in0=zt_t[i][:].rearrange("p t r -> p r t"),
                    in1=g_bc, op=ALU.mult,
                )
            elif kind == "Q":
                s, e = QUANTS[i]
                code_t[i] = gpool.tile([P, (e - s) * P], U32, name="codes", tag="codes", align_bytes=64)
                scale_t[i] = gpool.tile([P, (e - s) * P], U8, name="scales", tag="scales", align_bytes=64)
                nc.vector.quantize_mx(
                    out=code_t[i][:].bitcast(FP8X4),
                    scales=scale_t[i][:],
                    in_=grp_t[i][:].rearrange("p a r t -> p (a r t)"),
                )
            elif kind == "M":
                n, j = quant_of[i]
                ob_t[i] = psum.tile([P, E], F32, name="ob", tag="ob")
                nc.tensor.matmul_mx(
                    out=ob_t[i][:],
                    lhsT=code_t[n][:, P * j : P * j + P].bitcast(FP8X4),
                    lhsT_scale=scale_t[n][:, P * j : P * j + P],
                    rhs=w_codes[:].bitcast(FP8X4),
                    rhs_scale=w_scales[:],
                    start=True,
                    stop=True,
                )
            elif kind == "O":
                n, j = store_of[i]
                if n not in osb_t:
                    s, e = STORES[n]
                    osb_t[n] = opool.tile([P, e - s, E], F32, name="osb", tag="osb")
                if eng == "S":
                    nc.scalar.copy(out=osb_t[n][:, j, :], in_=ob_t[i][:])
                else:
                    nc.vector.tensor_copy(out=osb_t[n][:, j, :], in_=ob_t[i][:])
            elif kind == "ST":
                s, e = STORES[i]
                c, j0 = divmod(s, CH)
                nc.sync.dma_start(out=out_view[c][:, j0 : j0 + e - s, :], in_=osb_t[i][:])
